import numpy as np
import ml_dtypes


def mxq(x, axis, fmt="e4m3"):
    dtype, down = {"e4m3": (ml_dtypes.float8_e4m3fn, 7), "e5m2": (ml_dtypes.float8_e5m2, 14)}[fmt]
    v = np.moveaxis(np.asarray(x, np.float32).astype(ml_dtypes.bfloat16).astype(np.float64), axis, -1)
    blocks = v.reshape(v.shape[:-1] + (-1, 32))
    amax = np.abs(blocks).max(-1, keepdims=True)
    byte = np.maximum(np.where(amax > 0, np.frexp(amax)[1] - 1 + 127, 0) - down, 1)
    scale = np.exp2(byte - 127.0)
    codes = (blocks / scale).astype(np.float32).astype(dtype).astype(np.float64)
    return np.moveaxis((codes * scale).reshape(v.shape), -1, axis)


WIDE = False


def mx_kscale(k):
    if not WIDE:
        return np.ones(k)
    levels = np.array([10, -10, 5, -5, 0])
    a = np.random.permutation(np.resize(levels, k // 512 * 4)).reshape(k // 512, 4)
    idx = np.arange(k)
    return np.exp2(a[idx // 512, idx % 128 // 32])


BF16 = ml_dtypes.bfloat16


def bf(x):
    return np.asarray(x, np.float32).astype(BF16)


def f64(x):
    return np.asarray(x).astype(np.float64)


B, S, D, BD, K = 4, 1024, 1024, 512, 128
TS = 3.0


def sigmoid(v):
    return 1.0 / (1.0 + np.exp(-v))


def setup_inputs():
    s = mx_kscale(D)
    return {
        "token_embeddings": bf(np.random.standard_normal((B, S, D)) * TS * s),
        "splat_influences": bf(np.random.uniform(size=(B, S, K))),
        "decoded": bf(np.random.standard_normal((B, K, D)) * 0.35),
        "gate_W": bf(np.random.standard_normal((D, D)) / (TS * np.sqrt(D)) / s[:, None]),
        "gate_b": bf(np.random.standard_normal(D) * 0.5),
    }


def reference(token_embeddings, splat_influences, decoded, gate_W, gate_b):
    flow = f64(splat_influences) @ f64(decoded)
    gate = sigmoid((mxq(f64(token_embeddings), 2, "e4m3") @ mxq(f64(gate_W), 0, "e4m3")) + f64(gate_b))
    return flow * gate

@@ -1,0 +1,288 @@
+from contextlib import ExitStack
+
+import concourse.masks as masks
+import concourse.mybir as mybir
+
+F32 = mybir.dt.float32
+BF16 = mybir.dt.bfloat16
+U32 = mybir.dt.uint32
+U8 = mybir.dt.uint8
+I32 = mybir.dt.int32
+FP8X4 = mybir.dt.float8_e4m3fn_x4
+ALU = mybir.AluOpType
+ACT = mybir.ActivationFunctionType
+
+P = 128
+NB = 4
+J = 8
+NT = NB * J
+D = 1024
+H = 512
+FLOPS = 2 * 4096 * 1024 * 1024 + 2 * 4096 * 128 * 1024
+
+MANUAL = True
+LT = 4
+LF = 2
+AF = 2
+AS = 1
+PRE = 2
+NOG = (NT - 1,)
+VSPLIT = 336
+
+
+def t_period(i):
+    return max(i - LT, (i - PRE) // 2)
+
+
+def f_period(i):
+    return max(i - LF, i // 2)
+
+
+def tile_splatinformationflow_pb_kernel(tc, token_embeddings, splat_influences, decoded, gate_W, gate_b, out):
+    nc = tc.nc
+    x_dram = token_embeddings.rearrange("b (p j) k -> b p (j k)", j=J)
+    i_dram = splat_influences.rearrange("b (p j) s -> b p (j s)", j=J)
+    o_dram = out.rearrange("b (p j) f -> b p (j f)", j=J)
+    w_dram = gate_W.rearrange("(c p e) n -> c p e n", c=4, e=2)
+    b_dram = gate_b.rearrange("(o n) -> o n", o=1)
+
+    with ExitStack() as ctx:
+        keep = ctx.enter_context(tc.tile_pool(name="keep", bufs=1))
+        xgp = ctx.enter_context(tc.tile_pool(name="xgp", bufs=3))
+        zp = ctx.enter_context(tc.tile_pool(name="zp", bufs=5))
+        fcp = ctx.enter_context(tc.tile_pool(name="fcp", bufs=6))
+        op = ctx.enter_context(tc.tile_pool(name="op", bufs=4))
+        ps_tp = ctx.enter_context(tc.psum_pool(name="ps_tp", bufs=3))
+        ps_v = ctx.enter_context(tc.psum_pool(name="ps_v", bufs=2))
+        ps_f = ctx.enter_context(tc.psum_pool(name="ps_f", bufs=2))
+        ps_g = ctx.enter_context(tc.psum_pool(name="ps_g", bufs=1))
+        if MANUAL:
+            ctx.enter_context(tc.manual_schedule())
+
+        x_sb = [keep.tile([P, J * D], BF16, name="x%d" % b) for b in range(NB)]
+        i_sb = [keep.tile([P, J * P], BF16, name="i%d" % b) for b in range(NB)]
+        iT_sb = [keep.tile([P, J * P], BF16, name="iT%d" % b) for b in range(NB)]
+        d_sb = [keep.tile([P, D], BF16, name="d%d" % b) for b in range(NB)]
+        wraw = keep.tile([P, 8, D], BF16, name="wraw")
+        wgrp = keep.tile([P, 8 * D], BF16, name="wgrp", align_bytes=64)
+        wc = keep.tile([P, 2 * D], U32, name="wc", align_bytes=64)
+        ws = keep.tile([P, 2 * D], U8, name="ws", align_bytes=64)
+        brow = keep.tile([P, D], BF16, name="brow")
+        ones = keep.tile([P, P], BF16, name="ones")
+        bias = keep.tile([P, D], F32, name="bias")
+        idf = keep.tile([P, P], F32, name="idf")
+        idb = keep.tile([P, P], BF16, name="idb")
+        dm = keep.tile([P, 8], F32, name="dm")
+        dm2 = keep.tile([P, 8], F32, name="dm2")
+
+        state = {}
+
+        def load_w(c, h):
+            nc.sync.dma_start(out=wraw[:, 2 * c:2 * c + 2, h * H:(h + 1) * H], in_=w_dram[c, :, :, h * H:(h + 1) * H])
+
+        def load_x(i0, n):
+            b, j = divmod(i0, J)
+            nc.sync.dma_start(out=x_sb[b][:, j * D:(j + n) * D], in_=x_dram[b, :, j * D:(j + n) * D])
+
+        def load_small(b):
+            nc.sync.dma_start(out=i_sb[b][:], in_=i_dram[b])
+            nc.sync.dma_start(out=d_sb[b][:], in_=decoded[b])
+
+        def regroup_w(g, h):
+            base = (2 * h + g) * 2048
+            for lo, hi, eng in ((0, VSPLIT, "v"), (VSPLIT, H, "s")):
+                dst = wgrp[:, base + 4 * lo:base + 4 * hi].rearrange("p (c i t) -> p c t i", i=4, t=4)
+                src = wraw[:, 4 * g:4 * g + 4, h * H + lo:h * H + hi].rearrange("p t (c i) -> p c t i", i=4)
+                if eng == "v":
+                    nc.vector.tensor_copy(out=dst, in_=src)
+                else:
+                    nc.scalar.copy(out=dst, in_=src)
+
+        def quant_w(h):
+            nc.vector.quantize_mx(
+                out=wc[:, h * D:(h + 1) * D].bitcast(FP8X4),
+                scales=ws[:, h * D:(h + 1) * D],
+                in_=wgrp[:, h * 4096:(h + 1) * 4096],
+            )
+
+        def transposes(i, cs):
+            b, j = divmod(i, J)
+            if 0 in cs:
+                xt = ps_tp.tile([P, 4, P], F32, name="xt", tag="tp")
+                state[("xt", i)] = xt
+            xt = state[("xt", i)]
+            xw = x_sb[b][:].bitcast(F32)
+            for c in cs:
+                nc.tensor.transpose(xt[:, c, :], xw[:, j * H + c * P:j * H + (c + 1) * P], idf[:])
+
+        def exit_x(i):
+            xg = xgp.tile([P, D], BF16, name="xg", tag="xg", align_bytes=64)
+            state[("xg", i)] = xg
+            nc.scalar.copy(
+                out=xg[:].bitcast(F32).rearrange("p (g r u) -> p g r u", g=2, u=2),
+                in_=state[("xt", i)][:].rearrange("p (g u) r -> p g r u", u=2),
+            )
+
+        def quant_x(i):
+            xc = xgp.tile([P, 256], U32, name="xc", tag="xc", align_bytes=64)
+            xs = xgp.tile([P, 256], U8, name="xs", tag="xs", align_bytes=64)
+            state[("xc", i)] = (xc, xs)
+            nc.vector.quantize_mx(out=xc[:].bitcast(FP8X4), scales=xs[:], in_=state[("xg", i)][:])
+
+        def infl_T(b, on_vector):
+            it = ps_tp.tile([P, J * P], BF16, name="it", tag="tp")
+            for j in range(J):
+                nc.tensor.transpose(it[:, j * P:(j + 1) * P], i_sb[b][:, j * P:(j + 1) * P], idb[:])
+            if on_vector:
+                nc.vector.tensor_copy(out=iT_sb[b][:], in_=it[:])
+            else:
+                nc.scalar.copy(out=iT_sb[b][:], in_=it[:])
+
+        def mx(i, h):
+            xc, xs = state[("xc", i)]
+            v = ps_v.tile([P, H], F32, name="v", tag="v")
+            state[("v", i, h)] = v
+            for g in range(2):
+                r = h * D + g * H
+                nc.tensor.matmul_mx(
+                    out=v[:],
+                    lhsT=xc[:, g * P:(g + 1) * P].bitcast(FP8X4),
+                    lhsT_scale=xs[:, g * P:(g + 1) * P],
+                    rhs=wc[:, r:r + H].bitcast(FP8X4),
+                    rhs_scale=ws[:, r:r + H],
+                    start=(g == 0),
+                    stop=(g == 1),
+                )
+
+        def add_bias(i, h):
+            if h == 0:
+                z = zp.tile([P, D], F32, name="z", tag="z")
+                state[("z", i)] = z
+            z = state[("z", i)]
+            nc.vector.tensor_tensor(out=z[:, h * H:(h + 1) * H], in0=state[("v", i, h)][:], in1=bias[:, h * H:(h + 1) * H], op=ALU.add)
+
+        def sigmoid(i):
+            z = state[("z", i)]
+            nc.scalar.activation(out=z[:], in_=z[:], func=ACT.Sigmoid)
+
+        def flow(i, h, pool, tag):
+            b, j = divmod(i, J)
+            f = pool.tile([P, H], F32, name=tag, tag=tag)
+            state[("f", i, h)] = f
+            nc.tensor.matmul(out=f[:], lhsT=iT_sb[b][:, j * P:(j + 1) * P], rhs=d_sb[b][:, h * H:(h + 1) * H], start=True, stop=True)
+
+        def flow_copy(i):
+            fc = fcp.tile([P, H], F32, name="fc", tag="fc")
+            state[("fc", i)] = fc
+            nc.scalar.copy(out=fc[:], in_=state[("f", i, 1)][:])
+
+        def mult_v(i, h):
+            if h == 0:
+                o = op.tile([P, D], F32, name="o", tag="o")
+                state[("o", i)] = o
+            o = state[("o", i)]
+            nc.vector.tensor_tensor(out=o[:, h * H:(h + 1) * H], in0=state[("f", i, h)][:], in1=state[("z", i)][:, h * H:(h + 1) * H], op=ALU.mult)
+
+        def mult_g(i):
+            o = state[("o", i)]
+            nc.gpsimd.tensor_tensor(out=o[:, H:D], in0=state[("z", i)][:, H:D], in1=state[("fc", i)][:], op=ALU.mult)
+
+        def store(i, lo, hi):
+            b, j = divmod(i, J)
+            nc.sync.dma_start(out=o_dram[b, :, j * D + lo:j * D + hi], in_=state[("o", i)][:, lo:hi])
+
+        nc.vector.memset(brow[:].bitcast(I32), 0)
+        nc.vector.memset(ones[:], 1.0)
+        nc.vector.memset(dm[:], 0.0)
+        nc.scalar.dma_start(out=brow[0:1, :], in_=b_dram)
+        nc.scalar.activation(out=dm2[:], in_=dm[:], func=ACT.Sigmoid)
+        masks.make_identity(nc, idf[:])
+        masks.make_identity(nc, idb[:])
+        for c in range(4):
+            load_w(c, 0)
+        load_x(0, 1)
+        for c in range(4):
+            load_w(c, 1)
+        load_x(1, 1)
+        load_small(0)
+        load_x(2, 2)
+        load_x(4, 4)
+        load_x(8, 4)
+        load_small(1)
+
+        for h in range(2):
+            bp = ps_v.tile([P, H], F32, name="bp", tag="v")
+            nc.tensor.matmul(out=bp[:], lhsT=ones[:], rhs=brow[:, h * H:(h + 1) * H], start=True, stop=True)
+            nc.scalar.copy(out=bias[:, h * H:(h + 1) * H], in_=bp[:])
+
+        regroup_w(0, 0)
+        regroup_w(1, 0)
+        transposes(0, [0, 1, 2, 3])
+        exit_x(0)
+        quant_w(0)
+        regroup_w(0, 1)
+        regroup_w(1, 1)
+        quant_x(0)
+        quant_w(1)
+        transposes(1, [0, 1, 2, 3])
+        exit_x(1)
+        infl_T(0, False)
+        quant_x(1)
+
+        for t in range(NT + AF):
+            u = t - AF
+            has_m = 0 <= u < NT
+            on_g = has_m and u not in NOG
+            sg = t - AS
+            ts = [i for i in range(PRE, NT) if t_period(i) == t]
+            es = [i for i in range(PRE, NT) if t_period(i) + 1 == t]
+            fs = [i for i in range(NT) if f_period(i) == t and i not in NOG]
+            if t < NT:
+                mx(t, 0)
+                mx(t, 1)
+            if has_m:
+                flow(u, 0, ps_f, "f")
+                if not on_g:
+                    flow(u, 1, ps_f, "f")
+            if ts:
+                transposes(ts[0], [0, 1])
+            if fs:
+                flow(fs[0], 1, ps_g, "fg")
+            if ts:
+                transposes(ts[0], [2, 3])
+            for i in ts[1:]:
+                transposes(i, [0, 1, 2, 3])
+            if t < NT:
+                add_bias(t, 0)
+                add_bias(t, 1)
+            for i in es:
+                exit_x(i)
+            if fs:
+                flow_copy(fs[0])
+            if 0 <= sg < NT:
+                sigmoid(sg)
+            for i in fs[1:]:
+                flow(i, 1, ps_g, "fg")
+                flow_copy(i)
+            if has_m:
+                mult_v(u, 0)
+                if u == NT - 1:
+                    store(u, 0, H)
+                if on_g:
+                    mult_g(u)
+                else:
+                    mult_v(u, 1)
+                if u == NT - 1:
+                    store(u, H, D)
+                else:
+                    store(u, 0, D)
+            if t % 4 == 0:
+                m = (t + 12) // 4
+                if m < NT // 4:
+                    load_x(4 * m, 4)
+                    if m % 2 == 0:
+                        load_small(m // 2)
+            if t % J == 2 and t // J + 1 < NB:
+                infl_T(t // J + 1, True)
+            for i in es:
+                quant_x(i)

@@ -27,6 +27,7 @@ AF = 2
 AS = 1
 PRE = 2
 NOG = (NT - 1,)
+BOTH = tuple(range(3, NT - 1, 4))
 VSPLIT = 336
 
 
@@ -50,7 +51,7 @@ def tile_splatinformationflow_pb_kernel(tc, token_embeddings, splat_influences, 
         keep = ctx.enter_context(tc.tile_pool(name="keep", bufs=1))
         xgp = ctx.enter_context(tc.tile_pool(name="xgp", bufs=3))
         zp = ctx.enter_context(tc.tile_pool(name="zp", bufs=5))
-        fcp = ctx.enter_context(tc.tile_pool(name="fcp", bufs=6))
+        fcp = ctx.enter_context(tc.tile_pool(name="fcp", bufs=8))
         op = ctx.enter_context(tc.tile_pool(name="op", bufs=4))
         ps_tp = ctx.enter_context(tc.psum_pool(name="ps_tp", bufs=3))
         ps_v = ctx.enter_context(tc.psum_pool(name="ps_v", bufs=2))
@@ -171,21 +172,18 @@ def tile_splatinformationflow_pb_kernel(tc, token_embeddings, splat_influences, 
             state[("f", i, h)] = f
             nc.tensor.matmul(out=f[:], lhsT=iT_sb[b][:, j * P:(j + 1) * P], rhs=d_sb[b][:, h * H:(h + 1) * H], start=True, stop=True)
 
-        def flow_copy(i):
+        def flow_copy(i, h):
             fc = fcp.tile([P, H], F32, name="fc", tag="fc")
-            state[("fc", i)] = fc
-            nc.scalar.copy(out=fc[:], in_=state[("f", i, 1)][:])
+            state[("fc", i, h)] = fc
+            nc.scalar.copy(out=fc[:], in_=state[("f", i, h)][:])
 
         def mult_v(i, h):
-            if h == 0:
-                o = op.tile([P, D], F32, name="o", tag="o")
-                state[("o", i)] = o
             o = state[("o", i)]
             nc.vector.tensor_tensor(out=o[:, h * H:(h + 1) * H], in0=state[("f", i, h)][:], in1=state[("z", i)][:, h * H:(h + 1) * H], op=ALU.mult)
 
-        def mult_g(i):
+        def mult_g(i, h):
             o = state[("o", i)]
-            nc.gpsimd.tensor_tensor(out=o[:, H:D], in0=state[("z", i)][:, H:D], in1=state[("fc", i)][:], op=ALU.mult)
+            nc.gpsimd.tensor_tensor(out=o[:, h * H:(h + 1) * H], in0=state[("z", i)][:, h * H:(h + 1) * H], in1=state[("fc", i, h)][:], op=ALU.mult)
 
         def store(i, lo, hi):
             b, j = divmod(i, J)
@@ -236,18 +234,20 @@ def tile_splatinformationflow_pb_kernel(tc, token_embeddings, splat_influences, 
             sg = t - AS
             ts = [i for i in range(PRE, NT) if t_period(i) == t]
             es = [i for i in range(PRE, NT) if t_period(i) + 1 == t]
-            fs = [i for i in range(NT) if f_period(i) == t and i not in NOG]
+            fs = [(i, 1) for i in range(NT) if f_period(i) == t and i not in NOG]
+            fs = fs + [(i, 0) for i in range(NT) if f_period(i) == t and i in BOTH]
             if t < NT:
                 mx(t, 0)
                 mx(t, 1)
             if has_m:
-                flow(u, 0, ps_f, "f")
+                if u not in BOTH:
+                    flow(u, 0, ps_f, "f")
                 if not on_g:
                     flow(u, 1, ps_f, "f")
             if ts:
                 transposes(ts[0], [0, 1])
             if fs:
-                flow(fs[0], 1, ps_g, "fg")
+                flow(fs[0][0], fs[0][1], ps_g, "fg")
             if ts:
                 transposes(ts[0], [2, 3])
             for i in ts[1:]:
@@ -258,18 +258,23 @@ def tile_splatinformationflow_pb_kernel(tc, token_embeddings, splat_influences, 
             for i in es:
                 exit_x(i)
             if fs:
-                flow_copy(fs[0])
+                flow_copy(fs[0][0], fs[0][1])
             if 0 <= sg < NT:
                 sigmoid(sg)
-            for i in fs[1:]:
-                flow(i, 1, ps_g, "fg")
-                flow_copy(i)
+            for i, h in fs[1:]:
+                flow(i, h, ps_g, "fg")
+                flow_copy(i, h)
             if has_m:
-                mult_v(u, 0)
+                o = op.tile([P, D], F32, name="o", tag="o")
+                state[("o", u)] = o
+                if u in BOTH:
+                    mult_g(u, 0)
+                else:
+                    mult_v(u, 0)
                 if u == NT - 1:
                     store(u, 0, H)
                 if on_g:
-                    mult_g(u)
+                    mult_g(u, 1)
                 else:
                     mult_v(u, 1)
                 if u == NT - 1:

@@ -27,7 +27,6 @@ AF = 2
 AS = 1
 PRE = 2
 NOG = (NT - 1,)
-BOTH = tuple(range(3, NT - 1, 4))
 VSPLIT = 336
 
 
@@ -51,7 +50,7 @@ def tile_splatinformationflow_pb_kernel(tc, token_embeddings, splat_influences, 
         keep = ctx.enter_context(tc.tile_pool(name="keep", bufs=1))
         xgp = ctx.enter_context(tc.tile_pool(name="xgp", bufs=3))
         zp = ctx.enter_context(tc.tile_pool(name="zp", bufs=5))
-        fcp = ctx.enter_context(tc.tile_pool(name="fcp", bufs=8))
+        fcp = ctx.enter_context(tc.tile_pool(name="fcp", bufs=6))
         op = ctx.enter_context(tc.tile_pool(name="op", bufs=4))
         ps_tp = ctx.enter_context(tc.psum_pool(name="ps_tp", bufs=3))
         ps_v = ctx.enter_context(tc.psum_pool(name="ps_v", bufs=2))
@@ -172,18 +171,21 @@ def tile_splatinformationflow_pb_kernel(tc, token_embeddings, splat_influences, 
             state[("f", i, h)] = f
             nc.tensor.matmul(out=f[:], lhsT=iT_sb[b][:, j * P:(j + 1) * P], rhs=d_sb[b][:, h * H:(h + 1) * H], start=True, stop=True)
 
-        def flow_copy(i, h):
+        def flow_copy(i):
             fc = fcp.tile([P, H], F32, name="fc", tag="fc")
-            state[("fc", i, h)] = fc
-            nc.scalar.copy(out=fc[:], in_=state[("f", i, h)][:])
+            state[("fc", i)] = fc
+            nc.scalar.copy(out=fc[:], in_=state[("f", i, 1)][:])
 
         def mult_v(i, h):
+            if h == 0:
+                o = op.tile([P, D], F32, name="o", tag="o")
+                state[("o", i)] = o
             o = state[("o", i)]
             nc.vector.tensor_tensor(out=o[:, h * H:(h + 1) * H], in0=state[("f", i, h)][:], in1=state[("z", i)][:, h * H:(h + 1) * H], op=ALU.mult)
 
-        def mult_g(i, h):
+        def mult_g(i):
             o = state[("o", i)]
-            nc.gpsimd.tensor_tensor(out=o[:, h * H:(h + 1) * H], in0=state[("z", i)][:, h * H:(h + 1) * H], in1=state[("fc", i, h)][:], op=ALU.mult)
+            nc.gpsimd.tensor_tensor(out=o[:, H:D], in0=state[("z", i)][:, H:D], in1=state[("fc", i)][:], op=ALU.mult)
 
         def store(i, lo, hi):
             b, j = divmod(i, J)
@@ -234,47 +236,36 @@ def tile_splatinformationflow_pb_kernel(tc, token_embeddings, splat_influences, 
             sg = t - AS
             ts = [i for i in range(PRE, NT) if t_period(i) == t]
             es = [i for i in range(PRE, NT) if t_period(i) + 1 == t]
-            fs = [(i, 1) for i in range(NT) if f_period(i) == t and i not in NOG]
-            fs = fs + [(i, 0) for i in range(NT) if f_period(i) == t and i in BOTH]
+            fs = [i for i in range(NT) if f_period(i) == t and i not in NOG]
             if t < NT:
                 mx(t, 0)
                 mx(t, 1)
             if has_m:
-                if u not in BOTH:
-                    flow(u, 0, ps_f, "f")
+                flow(u, 0, ps_f, "f")
                 if not on_g:
                     flow(u, 1, ps_f, "f")
-            if ts:
-                transposes(ts[0], [0, 1])
-            if fs:
-                flow(fs[0][0], fs[0][1], ps_g, "fg")
-            if ts:
-                transposes(ts[0], [2, 3])
-            for i in ts[1:]:
+            for i in ts:
                 transposes(i, [0, 1, 2, 3])
+            if fs:
+                flow(fs[0], 1, ps_g, "fg")
             if t < NT:
                 add_bias(t, 0)
                 add_bias(t, 1)
             for i in es:
                 exit_x(i)
             if fs:
-                flow_copy(fs[0][0], fs[0][1])
+                flow_copy(fs[0])
             if 0 <= sg < NT:
                 sigmoid(sg)
-            for i, h in fs[1:]:
-                flow(i, h, ps_g, "fg")
-                flow_copy(i, h)
+            for i in fs[1:]:
+                flow(i, 1, ps_g, "fg")
+                flow_copy(i)
             if has_m:
-                o = op.tile([P, D], F32, name="o", tag="o")
-                state[("o", u)] = o
-                if u in BOTH:
-                    mult_g(u, 0)
-                else:
-                    mult_v(u, 0)
+                mult_v(u, 0)
                 if u == NT - 1:
                     store(u, 0, H)
                 if on_g:
-                    mult_g(u, 1)
+                    mult_g(u)
                 else:
                     mult_v(u, 1)
                 if u == NT - 1:

@@ -161,9 +161,9 @@ def tile_splatinformationflow_pb_kernel(tc, token_embeddings, splat_influences, 
             z = state[("z", i)]
             nc.vector.tensor_tensor(out=z[:, h * H:(h + 1) * H], in0=state[("v", i, h)][:], in1=bias[:, h * H:(h + 1) * H], op=ALU.add)
 
-        def sigmoid(i):
+        def sigmoid(i, lo, hi):
             z = state[("z", i)]
-            nc.scalar.activation(out=z[:], in_=z[:], func=ACT.Sigmoid)
+            nc.scalar.activation(out=z[:, lo:hi], in_=z[:, lo:hi], func=ACT.Sigmoid)
 
         def flow(i, h, pool, tag):
             b, j = divmod(i, J)
@@ -210,11 +210,6 @@ def tile_splatinformationflow_pb_kernel(tc, token_embeddings, splat_influences, 
         load_x(8, 4)
         load_small(1)
 
-        for h in range(2):
-            bp = ps_v.tile([P, H], F32, name="bp", tag="v")
-            nc.tensor.matmul(out=bp[:], lhsT=ones[:], rhs=brow[:, h * H:(h + 1) * H], start=True, stop=True)
-            nc.scalar.copy(out=bias[:, h * H:(h + 1) * H], in_=bp[:])
-
         regroup_w(0, 0)
         regroup_w(1, 0)
         transposes(0, [0, 1, 2, 3])
@@ -224,6 +219,10 @@ def tile_splatinformationflow_pb_kernel(tc, token_embeddings, splat_influences, 
         regroup_w(1, 1)
         quant_x(0)
         quant_w(1)
+        for h in range(2):
+            bp = ps_v.tile([P, H], F32, name="bp", tag="v")
+            nc.tensor.matmul(out=bp[:], lhsT=ones[:], rhs=brow[:, h * H:(h + 1) * H], start=True, stop=True)
+            nc.scalar.copy(out=bias[:, h * H:(h + 1) * H], in_=bp[:])
         transposes(1, [0, 1, 2, 3])
         exit_x(1)
         infl_T(0, False)
@@ -244,10 +243,14 @@ def tile_splatinformationflow_pb_kernel(tc, token_embeddings, splat_influences, 
                 flow(u, 0, ps_f, "f")
                 if not on_g:
                     flow(u, 1, ps_f, "f")
-            for i in ts:
-                transposes(i, [0, 1, 2, 3])
+            if ts:
+                transposes(ts[0], [0, 1])
             if fs:
                 flow(fs[0], 1, ps_g, "fg")
+            if ts:
+                transposes(ts[0], [2, 3])
+            for i in ts[1:]:
+                transposes(i, [0, 1, 2, 3])
             if t < NT:
                 add_bias(t, 0)
                 add_bias(t, 1)
@@ -255,8 +258,11 @@ def tile_splatinformationflow_pb_kernel(tc, token_embeddings, splat_influences, 
                 exit_x(i)
             if fs:
                 flow_copy(fs[0])
-            if 0 <= sg < NT:
-                sigmoid(sg)
+            if 0 <= sg < NT - 1:
+                sigmoid(sg, 0, D)
+            if t == NT - 1:
+                sigmoid(t, 0, H)
+                sigmoid(t, H, D)
             for i in fs[1:]:
                 flow(i, 1, ps_g, "fg")
                 flow_copy(i)

@@ -243,12 +243,10 @@ def tile_splatinformationflow_pb_kernel(tc, token_embeddings, splat_influences, 
                 flow(u, 0, ps_f, "f")
                 if not on_g:
                     flow(u, 1, ps_f, "f")
-            if ts:
-                transposes(ts[0], [0, 1])
             if fs:
                 flow(fs[0], 1, ps_g, "fg")
             if ts:
-                transposes(ts[0], [2, 3])
+                transposes(ts[0], [0, 1, 2, 3])
             for i in ts[1:]:
                 transposes(i, [0, 1, 2, 3])
             if t < NT:

@@ -27,6 +27,7 @@ AF = 2
 AS = 1
 PRE = 2
 NOG = (NT - 1,)
+VTP = (NT - 2,)
 VSPLIT = 336
 
 
@@ -140,7 +141,10 @@ def tile_splatinformationflow_pb_kernel(tc, token_embeddings, splat_influences, 
 
         def mx(i, h):
             xc, xs = state[("xc", i)]
-            v = ps_v.tile([P, H], F32, name="v", tag="v")
+            if i in VTP:
+                v = ps_tp.tile([P, H], F32, name="vt", tag="tp")
+            else:
+                v = ps_v.tile([P, H], F32, name="v", tag="v")
             state[("v", i, h)] = v
             for g in range(2):
                 r = h * D + g * H
@@ -239,12 +243,16 @@ def tile_splatinformationflow_pb_kernel(tc, token_embeddings, splat_influences, 
             if t < NT:
                 mx(t, 0)
                 mx(t, 1)
-            if has_m:
+            if has_m and u < NT - 2:
                 flow(u, 0, ps_f, "f")
-                if not on_g:
-                    flow(u, 1, ps_f, "f")
+            if t == NT - 1:
+                flow(NT - 2, 0, ps_f, "f")
+                flow(NT - 1, 0, ps_tp, "tp")
+                flow(NT - 1, 1, ps_g, "fg")
             if fs:
                 flow(fs[0], 1, ps_g, "fg")
+            for i in fs[1:]:
+                flow(i, 1, ps_f, "f")
             if ts:
                 transposes(ts[0], [0, 1, 2, 3])
             for i in ts[1:]:
@@ -262,7 +270,6 @@ def tile_splatinformationflow_pb_kernel(tc, token_embeddings, splat_influences, 
                 sigmoid(t, 0, H)
                 sigmoid(t, H, D)
             for i in fs[1:]:
-                flow(i, 1, ps_g, "fg")
                 flow_copy(i)
             if has_m:
                 mult_v(u, 0)

@@ -53,10 +53,11 @@ def tile_splatinformationflow_pb_kernel(tc, token_embeddings, splat_influences, 
         zp = ctx.enter_context(tc.tile_pool(name="zp", bufs=5))
         fcp = ctx.enter_context(tc.tile_pool(name="fcp", bufs=6))
         op = ctx.enter_context(tc.tile_pool(name="op", bufs=4))
-        ps_tp = ctx.enter_context(tc.psum_pool(name="ps_tp", bufs=3))
-        ps_v = ctx.enter_context(tc.psum_pool(name="ps_v", bufs=2))
-        ps_f = ctx.enter_context(tc.psum_pool(name="ps_f", bufs=2))
-        ps_g = ctx.enter_context(tc.psum_pool(name="ps_g", bufs=1))
+        ps = ctx.enter_context(tc.psum_pool(name="ps", bufs=8))
+        ps_tp = ps
+        ps_v = ps
+        ps_f = ps
+        ps_g = ps
         if MANUAL:
             ctx.enter_context(tc.manual_schedule())
 
@@ -109,7 +110,7 @@ def tile_splatinformationflow_pb_kernel(tc, token_embeddings, splat_influences, 
         def transposes(i, cs):
             b, j = divmod(i, J)
             if 0 in cs:
-                xt = ps_tp.tile([P, 4, P], F32, name="xt", tag="tp")
+                xt = ps_tp.tile([P, 4, P], F32, name="xt", tag="b")
                 state[("xt", i)] = xt
             xt = state[("xt", i)]
             xw = x_sb[b][:].bitcast(F32)
@@ -131,7 +132,7 @@ def tile_splatinformationflow_pb_kernel(tc, token_embeddings, splat_influences, 
             nc.vector.quantize_mx(out=xc[:].bitcast(FP8X4), scales=xs[:], in_=state[("xg", i)][:])
 
         def infl_T(b, on_vector):
-            it = ps_tp.tile([P, J * P], BF16, name="it", tag="tp")
+            it = ps_tp.tile([P, J * P], BF16, name="it", tag="b")
             for j in range(J):
                 nc.tensor.transpose(it[:, j * P:(j + 1) * P], i_sb[b][:, j * P:(j + 1) * P], idb[:])
             if on_vector:
@@ -142,9 +143,9 @@ def tile_splatinformationflow_pb_kernel(tc, token_embeddings, splat_influences, 
         def mx(i, h):
             xc, xs = state[("xc", i)]
             if i in VTP:
-                v = ps_tp.tile([P, H], F32, name="vt", tag="tp")
+                v = ps_tp.tile([P, H], F32, name="vt", tag="b")
             else:
-                v = ps_v.tile([P, H], F32, name="v", tag="v")
+                v = ps_v.tile([P, H], F32, name="v", tag="b")
             state[("v", i, h)] = v
             for g in range(2):
                 r = h * D + g * H
@@ -171,7 +172,7 @@ def tile_splatinformationflow_pb_kernel(tc, token_embeddings, splat_influences, 
 
         def flow(i, h, pool, tag):
             b, j = divmod(i, J)
-            f = pool.tile([P, H], F32, name=tag, tag=tag)
+            f = pool.tile([P, H], F32, name=tag, tag="b")
             state[("f", i, h)] = f
             nc.tensor.matmul(out=f[:], lhsT=iT_sb[b][:, j * P:(j + 1) * P], rhs=d_sb[b][:, h * H:(h + 1) * H], start=True, stop=True)
 
@@ -224,7 +225,7 @@ def tile_splatinformationflow_pb_kernel(tc, token_embeddings, splat_influences, 
         quant_x(0)
         quant_w(1)
         for h in range(2):
-            bp = ps_v.tile([P, H], F32, name="bp", tag="v")
+            bp = ps_v.tile([P, H], F32, name="bp", tag="b")
             nc.tensor.matmul(out=bp[:], lhsT=ones[:], rhs=brow[:, h * H:(h + 1) * H], start=True, stop=True)
             nc.scalar.copy(out=bias[:, h * H:(h + 1) * H], in_=bp[:])
         transposes(1, [0, 1, 2, 3])

@@ -26,7 +26,7 @@ LF = 2
 AF = 2
 AS = 1
 PRE = 2
-NOG = (NT - 1,)
+NOG = (7, 15, 23, NT - 1)
 VTP = (NT - 2,)
 VSPLIT = 336
 
@@ -246,6 +246,8 @@ def tile_splatinformationflow_pb_kernel(tc, token_embeddings, splat_influences, 
                 mx(t, 1)
             if has_m and u < NT - 2:
                 flow(u, 0, ps_f, "f")
+                if not on_g:
+                    flow(u, 1, ps_f, "f")
             if t == NT - 1:
                 flow(NT - 2, 0, ps_f, "f")
                 flow(NT - 1, 0, ps_tp, "tp")

@@ -31,8 +31,12 @@ VTP = (NT - 2,)
 VSPLIT = 336
 
 
+def e_period(i):
+    return max(i - LT, (i - PRE) // 2) + 1
+
+
 def t_period(i):
-    return max(i - LT, (i - PRE) // 2)
+    return e_period(i - i % 2) - 1
 
 
 def f_period(i):
@@ -49,7 +53,7 @@ def tile_splatinformationflow_pb_kernel(tc, token_embeddings, splat_influences, 
 
     with ExitStack() as ctx:
         keep = ctx.enter_context(tc.tile_pool(name="keep", bufs=1))
-        xgp = ctx.enter_context(tc.tile_pool(name="xgp", bufs=3))
+        xgp = ctx.enter_context(tc.tile_pool(name="xgp", bufs=4))
         zp = ctx.enter_context(tc.tile_pool(name="zp", bufs=5))
         fcp = ctx.enter_context(tc.tile_pool(name="fcp", bufs=6))
         op = ctx.enter_context(tc.tile_pool(name="op", bufs=4))

@@ -25,7 +25,7 @@ LT = 4
 LF = 2
 AF = 2
 AS = 1
-PRE = 2
+PRE = 4
 NOG = (7, 15, 23, NT - 1)
 VTP = (NT - 2,)
 VSPLIT = 336
@@ -53,7 +53,7 @@ def tile_splatinformationflow_pb_kernel(tc, token_embeddings, splat_influences, 
 
     with ExitStack() as ctx:
         keep = ctx.enter_context(tc.tile_pool(name="keep", bufs=1))
-        xgp = ctx.enter_context(tc.tile_pool(name="xgp", bufs=4))
+        xgp = ctx.enter_context(tc.tile_pool(name="xgp", bufs=3))
         zp = ctx.enter_context(tc.tile_pool(name="zp", bufs=5))
         fcp = ctx.enter_context(tc.tile_pool(name="fcp", bufs=6))
         op = ctx.enter_context(tc.tile_pool(name="op", bufs=4))
@@ -69,13 +69,13 @@ def tile_splatinformationflow_pb_kernel(tc, token_embeddings, splat_influences, 
         i_sb = [keep.tile([P, J * P], BF16, name="i%d" % b) for b in range(NB)]
         iT_sb = [keep.tile([P, J * P], BF16, name="iT%d" % b) for b in range(NB)]
         d_sb = [keep.tile([P, D], BF16, name="d%d" % b) for b in range(NB)]
-        wraw = keep.tile([P, 8, D], BF16, name="wraw")
+        wraw = [keep.tile([P, 8, H], BF16, name="wraw%d" % h) for h in range(2)]
         wgrp = keep.tile([P, 8 * D], BF16, name="wgrp", align_bytes=64)
         wc = keep.tile([P, 2 * D], U32, name="wc", align_bytes=64)
         ws = keep.tile([P, 2 * D], U8, name="ws", align_bytes=64)
         brow = keep.tile([P, D], BF16, name="brow")
         ones = keep.tile([P, P], BF16, name="ones")
-        bias = keep.tile([P, D], F32, name="bias")
+        bias = keep.tile([P, D], BF16, name="bias")
         idf = keep.tile([P, P], F32, name="idf")
         idb = keep.tile([P, P], BF16, name="idb")
         dm = keep.tile([P, 8], F32, name="dm")
@@ -84,7 +84,7 @@ def tile_splatinformationflow_pb_kernel(tc, token_embeddings, splat_influences, 
         state = {}
 
         def load_w(c, h):
-            nc.sync.dma_start(out=wraw[:, 2 * c:2 * c + 2, h * H:(h + 1) * H], in_=w_dram[c, :, :, h * H:(h + 1) * H])
+            nc.sync.dma_start(out=wraw[h][:, 2 * c:2 * c + 2, :], in_=w_dram[c, :, :, h * H:(h + 1) * H])
 
         def load_x(i0, n):
             b, j = divmod(i0, J)
@@ -98,7 +98,7 @@ def tile_splatinformationflow_pb_kernel(tc, token_embeddings, splat_influences, 
             base = (2 * h + g) * 2048
             for lo, hi, eng in ((0, VSPLIT, "v"), (VSPLIT, H, "s")):
                 dst = wgrp[:, base + 4 * lo:base + 4 * hi].rearrange("p (c i t) -> p c t i", i=4, t=4)
-                src = wraw[:, 4 * g:4 * g + 4, h * H + lo:h * H + hi].rearrange("p t (c i) -> p c t i", i=4)
+                src = wraw[h][:, 4 * g:4 * g + 4, lo:hi].rearrange("p t (c i) -> p c t i", i=4)
                 if eng == "v":
                     nc.vector.tensor_copy(out=dst, in_=src)
                 else:
@@ -122,18 +122,26 @@ def tile_splatinformationflow_pb_kernel(tc, token_embeddings, splat_influences, 
                 nc.tensor.transpose(xt[:, c, :], xw[:, j * H + c * P:j * H + (c + 1) * P], idf[:])
 
         def exit_x(i):
-            xg = xgp.tile([P, D], BF16, name="xg", tag="xg", align_bytes=64)
-            state[("xg", i)] = xg
+            m, r = divmod(i, 2)
+            if r == 0:
+                xg = xgp.tile([P, 2 * D], BF16, name="xg", tag="xg", align_bytes=64)
+                xc = xgp.tile([P, 512], U32, name="xc", tag="xc", align_bytes=64)
+                xs = xgp.tile([P, 512], U8, name="xs", tag="xs", align_bytes=64)
+                state[("xq", m)] = (xg, xc, xs)
+            xg = state[("xq", m)][0]
             nc.scalar.copy(
-                out=xg[:].bitcast(F32).rearrange("p (g r u) -> p g r u", g=2, u=2),
+                out=xg[:, r * D:(r + 1) * D].bitcast(F32).rearrange("p (g r u) -> p g r u", g=2, u=2),
                 in_=state[("xt", i)][:].rearrange("p (g u) r -> p g r u", u=2),
             )
 
-        def quant_x(i):
-            xc = xgp.tile([P, 256], U32, name="xc", tag="xc", align_bytes=64)
-            xs = xgp.tile([P, 256], U8, name="xs", tag="xs", align_bytes=64)
-            state[("xc", i)] = (xc, xs)
-            nc.vector.quantize_mx(out=xc[:].bitcast(FP8X4), scales=xs[:], in_=state[("xg", i)][:])
+        def quant_x(i, n):
+            m, r = divmod(i, 2)
+            xg, xc, xs = state[("xq", m)]
+            nc.vector.quantize_mx(
+                out=xc[:, r * 256:(r + n) * 256].bitcast(FP8X4),
+                scales=xs[:, r * 256:(r + n) * 256],
+                in_=xg[:, r * D:(r + n) * D],
+            )
 
         def infl_T(b, on_vector):
             it = ps_tp.tile([P, J * P], BF16, name="it", tag="b")
@@ -145,7 +153,8 @@ def tile_splatinformationflow_pb_kernel(tc, token_embeddings, splat_influences, 
                 nc.scalar.copy(out=iT_sb[b][:], in_=it[:])
 
         def mx(i, h):
-            xc, xs = state[("xc", i)]
+            xc, xs = state[("xq", i // 2)][1:]
+            x0 = (i % 2) * 256
             if i in VTP:
                 v = ps_tp.tile([P, H], F32, name="vt", tag="b")
             else:
@@ -155,8 +164,8 @@ def tile_splatinformationflow_pb_kernel(tc, token_embeddings, splat_influences, 
                 r = h * D + g * H
                 nc.tensor.matmul_mx(
                     out=v[:],
-                    lhsT=xc[:, g * P:(g + 1) * P].bitcast(FP8X4),
-                    lhsT_scale=xs[:, g * P:(g + 1) * P],
+                    lhsT=xc[:, x0 + g * P:x0 + (g + 1) * P].bitcast(FP8X4),
+                    lhsT_scale=xs[:, x0 + g * P:x0 + (g + 1) * P],
                     rhs=wc[:, r:r + H].bitcast(FP8X4),
                     rhs_scale=ws[:, r:r + H],
                     start=(g == 0),
@@ -226,16 +235,21 @@ def tile_splatinformationflow_pb_kernel(tc, token_embeddings, splat_influences, 
         quant_w(0)
         regroup_w(0, 1)
         regroup_w(1, 1)
-        quant_x(0)
+        quant_x(0, 1)
         quant_w(1)
+        bp = ps_v.tile([P, D], BF16, name="bp", tag="b")
         for h in range(2):
-            bp = ps_v.tile([P, H], F32, name="bp", tag="b")
-            nc.tensor.matmul(out=bp[:], lhsT=ones[:], rhs=brow[:, h * H:(h + 1) * H], start=True, stop=True)
-            nc.scalar.copy(out=bias[:, h * H:(h + 1) * H], in_=bp[:])
+            nc.tensor.matmul(out=bp[:, h * H:(h + 1) * H], lhsT=ones[:], rhs=brow[:, h * H:(h + 1) * H], start=True, stop=True)
+        nc.vector.tensor_copy(out=bias[:], in_=bp[:])
         transposes(1, [0, 1, 2, 3])
         exit_x(1)
+        quant_x(1, 1)
         infl_T(0, False)
-        quant_x(1)
+        transposes(2, [0, 1, 2, 3])
+        transposes(3, [0, 1, 2, 3])
+        exit_x(2)
+        exit_x(3)
+        quant_x(2, 2)
 
         for t in range(NT + AF):
             u = t - AF
@@ -298,5 +312,5 @@ def tile_splatinformationflow_pb_kernel(tc, token_embeddings, splat_influences, 
                         load_small(m // 2)
             if t % J == 2 and t // J + 1 < NB:
                 infl_T(t // J + 1, True)
-            for i in es:
-                quant_x(i)
+            if es:
+                quant_x(es[0], 2)

@@ -25,6 +25,8 @@ LT = 4
 LF = 2
 AF = 2
 AS = 1
+TAIL = 3
+WU = (4, 1, 1)
 PRE = 4
 NOG = (7, 15, 23, NT - 1)
 VTP = (NT - 2,)
@@ -78,6 +80,7 @@ def tile_splatinformationflow_pb_kernel(tc, token_embeddings, splat_influences, 
         bias = keep.tile([P, D], BF16, name="bias")
         idf = keep.tile([P, P], F32, name="idf")
         idb = keep.tile([P, P], BF16, name="idb")
+        warm = keep.tile([P, H], BF16, name="warm")
         dm = keep.tile([P, 8], F32, name="dm")
         dm2 = keep.tile([P, 8], F32, name="dm2")
 
@@ -211,6 +214,7 @@ def tile_splatinformationflow_pb_kernel(tc, token_embeddings, splat_influences, 
 
         nc.vector.memset(brow[:].bitcast(I32), 0)
         nc.vector.memset(ones[:], 1.0)
+        nc.vector.memset(warm[:], 0.0)
         nc.vector.memset(dm[:], 0.0)
         nc.scalar.dma_start(out=brow[0:1, :], in_=b_dram)
         nc.scalar.activation(out=dm2[:], in_=dm[:], func=ACT.Sigmoid)
@@ -228,9 +232,15 @@ def tile_splatinformationflow_pb_kernel(tc, token_embeddings, splat_influences, 
         load_x(8, 4)
         load_small(1)
 
+        def warm_up(n):
+            wu = ps.tile([P, H], F32, name="wu", tag="b")
+            for q in range(n):
+                nc.tensor.matmul(out=wu[:], lhsT=ones[:], rhs=warm[:], start=True, stop=True)
+
         regroup_w(0, 0)
         regroup_w(1, 0)
         transposes(0, [0, 1, 2, 3])
+        warm_up(WU[0])
         exit_x(0)
         quant_w(0)
         regroup_w(0, 1)
@@ -242,9 +252,11 @@ def tile_splatinformationflow_pb_kernel(tc, token_embeddings, splat_influences, 
             nc.tensor.matmul(out=bp[:, h * H:(h + 1) * H], lhsT=ones[:], rhs=brow[:, h * H:(h + 1) * H], start=True, stop=True)
         nc.vector.tensor_copy(out=bias[:], in_=bp[:])
         transposes(1, [0, 1, 2, 3])
+        warm_up(WU[1])
         exit_x(1)
         quant_x(1, 1)
         infl_T(0, False)
+        warm_up(WU[2])
         transposes(2, [0, 1, 2, 3])
         transposes(3, [0, 1, 2, 3])
         exit_x(2)
@@ -259,6 +271,10 @@ def tile_splatinformationflow_pb_kernel(tc, token_embeddings, splat_influences, 
             ts = [i for i in range(PRE, NT) if t_period(i) == t]
             es = [i for i in range(PRE, NT) if t_period(i) + 1 == t]
             fs = [i for i in range(NT) if f_period(i) == t and i not in NOG]
+            if fs:
+                flow(fs[0], 1, ps_g, "fg")
+            for i in fs[1:]:
+                flow(i, 1, ps_f, "f")
             if t < NT:
                 mx(t, 0)
                 mx(t, 1)
@@ -270,10 +286,6 @@ def tile_splatinformationflow_pb_kernel(tc, token_embeddings, splat_influences, 
                 flow(NT - 2, 0, ps_f, "f")
                 flow(NT - 1, 0, ps_tp, "tp")
                 flow(NT - 1, 1, ps_g, "fg")
-            if fs:
-                flow(fs[0], 1, ps_g, "fg")
-            for i in fs[1:]:
-                flow(i, 1, ps_f, "f")
             if ts:
                 transposes(ts[0], [0, 1, 2, 3])
             for i in ts[1:]:
@@ -294,15 +306,17 @@ def tile_splatinformationflow_pb_kernel(tc, token_embeddings, splat_influences, 
                 flow_copy(i)
             if has_m:
                 mult_v(u, 0)
-                if u == NT - 1:
+                if u >= NT - TAIL:
                     store(u, 0, H)
+                if u > NT - TAIL:
+                    store(u - 1, H, D)
                 if on_g:
                     mult_g(u)
                 else:
                     mult_v(u, 1)
                 if u == NT - 1:
                     store(u, H, D)
-                else:
+                elif u < NT - TAIL:
                     store(u, 0, D)
             if t % 4 == 0:
                 m = (t + 12) // 4

@@ -26,7 +26,8 @@ LF = 2
 AF = 2
 AS = 1
 TAIL = 3
-WU = (4, 1, 1)
+WU = (10, 3)
+EF = 3
 PRE = 4
 NOG = (7, 15, 23, NT - 1)
 VTP = (NT - 2,)
@@ -107,11 +108,12 @@ def tile_splatinformationflow_pb_kernel(tc, token_embeddings, splat_influences, 
                 else:
                     nc.scalar.copy(out=dst, in_=src)
 
-        def quant_w(h):
+        def quant_w(g, h):
+            r = h * D + g * H
             nc.vector.quantize_mx(
-                out=wc[:, h * D:(h + 1) * D].bitcast(FP8X4),
-                scales=ws[:, h * D:(h + 1) * D],
-                in_=wgrp[:, h * 4096:(h + 1) * 4096],
+                out=wc[:, r:r + H].bitcast(FP8X4),
+                scales=ws[:, r:r + H],
+                in_=wgrp[:, 4 * r:4 * (r + H)],
             )
 
         def transposes(i, cs):
@@ -223,10 +225,10 @@ def tile_splatinformationflow_pb_kernel(tc, token_embeddings, splat_influences, 
         for c in range(4):
             load_w(c, 0)
         load_x(0, 1)
-        for c in range(4):
-            load_w(c, 1)
         load_x(1, 1)
         load_small(0)
+        for c in range(4):
+            load_w(c, 1)
         load_x(2, 2)
         load_x(4, 4)
         load_x(8, 4)
@@ -238,30 +240,44 @@ def tile_splatinformationflow_pb_kernel(tc, token_embeddings, splat_influences, 
                 nc.tensor.matmul(out=wu[:], lhsT=ones[:], rhs=warm[:], start=True, stop=True)
 
         regroup_w(0, 0)
+        quant_w(0, 0)
         regroup_w(1, 0)
-        transposes(0, [0, 1, 2, 3])
+        quant_w(1, 0)
         warm_up(WU[0])
+        transposes(0, [0, 1, 2, 3])
+        transposes(1, [0, 1, 2, 3])
         exit_x(0)
-        quant_w(0)
-        regroup_w(0, 1)
-        regroup_w(1, 1)
+        exit_x(1)
         quant_x(0, 1)
-        quant_w(1)
+        quant_x(1, 1)
+        infl_T(0, False)
         bp = ps_v.tile([P, D], BF16, name="bp", tag="b")
         for h in range(2):
             nc.tensor.matmul(out=bp[:, h * H:(h + 1) * H], lhsT=ones[:], rhs=brow[:, h * H:(h + 1) * H], start=True, stop=True)
-        nc.vector.tensor_copy(out=bias[:], in_=bp[:])
-        transposes(1, [0, 1, 2, 3])
+        mx(0, 0)
+        mx(1, 0)
+        for i in range(EF):
+            flow(i, 1, ps_f, "f")
         warm_up(WU[1])
-        exit_x(1)
-        quant_x(1, 1)
-        infl_T(0, False)
-        warm_up(WU[2])
+        nc.vector.tensor_copy(out=bias[:], in_=bp[:])
+        regroup_w(0, 1)
+        flow_copy(0)
+        regroup_w(1, 1)
+        quant_w(0, 1)
+        quant_w(1, 1)
         transposes(2, [0, 1, 2, 3])
         transposes(3, [0, 1, 2, 3])
+        add_bias(0, 0)
+        add_bias(1, 0)
         exit_x(2)
         exit_x(3)
+        for i in range(1, EF):
+            flow_copy(i)
+        mx(0, 1)
+        mx(1, 1)
         quant_x(2, 2)
+        add_bias(0, 1)
+        add_bias(1, 1)
 
         for t in range(NT + AF):
             u = t - AF
@@ -270,12 +286,12 @@ def tile_splatinformationflow_pb_kernel(tc, token_embeddings, splat_influences, 
             sg = t - AS
             ts = [i for i in range(PRE, NT) if t_period(i) == t]
             es = [i for i in range(PRE, NT) if t_period(i) + 1 == t]
-            fs = [i for i in range(NT) if f_period(i) == t and i not in NOG]
+            fs = [i for i in range(EF, NT) if f_period(i) == t and i not in NOG]
             if fs:
                 flow(fs[0], 1, ps_g, "fg")
             for i in fs[1:]:
                 flow(i, 1, ps_f, "f")
-            if t < NT:
+            if 2 <= t < NT:
                 mx(t, 0)
                 mx(t, 1)
             if has_m and u < NT - 2:
@@ -290,9 +306,12 @@ def tile_splatinformationflow_pb_kernel(tc, token_embeddings, splat_influences, 
                 transposes(ts[0], [0, 1, 2, 3])
             for i in ts[1:]:
                 transposes(i, [0, 1, 2, 3])
-            if t < NT:
+            if 2 <= t < NT:
                 add_bias(t, 0)
                 add_bias(t, 1)
+            for i in range(PRE, NT, 2):
+                if t_period(i) + 2 == t:
+                    quant_x(i, 2)
             for i in es:
                 exit_x(i)
             if fs:
@@ -326,5 +345,3 @@ def tile_splatinformationflow_pb_kernel(tc, token_embeddings, splat_influences, 
                         load_small(m // 2)
             if t % J == 2 and t // J + 1 < NB:
                 infl_T(t // J + 1, True)
-            if es:
-                quant_x(es[0], 2)

@@ -59,7 +59,7 @@ def tile_splatinformationflow_pb_kernel(tc, token_embeddings, splat_influences, 
         xgp = ctx.enter_context(tc.tile_pool(name="xgp", bufs=3))
         zp = ctx.enter_context(tc.tile_pool(name="zp", bufs=5))
         fcp = ctx.enter_context(tc.tile_pool(name="fcp", bufs=6))
-        op = ctx.enter_context(tc.tile_pool(name="op", bufs=4))
+        op = ctx.enter_context(tc.tile_pool(name="op", bufs=6))
         ps = ctx.enter_context(tc.psum_pool(name="ps", bufs=8))
         ps_tp = ps
         ps_v = ps
@@ -222,15 +222,21 @@ def tile_splatinformationflow_pb_kernel(tc, token_embeddings, splat_influences, 
         nc.scalar.activation(out=dm2[:], in_=dm[:], func=ACT.Sigmoid)
         masks.make_identity(nc, idf[:])
         masks.make_identity(nc, idb[:])
-        for c in range(4):
-            load_w(c, 0)
+        load_w(0, 0)
+        load_w(1, 0)
+        load_w(2, 0)
+        load_w(3, 0)
         load_x(0, 1)
         load_x(1, 1)
         load_small(0)
-        for c in range(4):
-            load_w(c, 1)
-        load_x(2, 2)
-        load_x(4, 4)
+        load_w(0, 1)
+        load_w(1, 1)
+        load_w(2, 1)
+        load_w(3, 1)
+        load_x(2, 1)
+        load_x(3, 1)
+        load_x(4, 2)
+        load_x(6, 2)
         load_x(8, 4)
         load_small(1)
 
@@ -245,15 +251,16 @@ def tile_splatinformationflow_pb_kernel(tc, token_embeddings, splat_influences, 
         quant_w(1, 0)
         warm_up(WU[0])
         transposes(0, [0, 1, 2, 3])
+        warm_up(1)
         transposes(1, [0, 1, 2, 3])
+        bp = ps_v.tile([P, D], BF16, name="bp", tag="b")
+        for h in range(2):
+            nc.tensor.matmul(out=bp[:, h * H:(h + 1) * H], lhsT=ones[:], rhs=brow[:, h * H:(h + 1) * H], start=True, stop=True)
         exit_x(0)
         exit_x(1)
         quant_x(0, 1)
         quant_x(1, 1)
         infl_T(0, False)
-        bp = ps_v.tile([P, D], BF16, name="bp", tag="b")
-        for h in range(2):
-            nc.tensor.matmul(out=bp[:, h * H:(h + 1) * H], lhsT=ones[:], rhs=brow[:, h * H:(h + 1) * H], start=True, stop=True)
         mx(0, 0)
         mx(1, 0)
         for i in range(EF):
@@ -261,17 +268,18 @@ def tile_splatinformationflow_pb_kernel(tc, token_embeddings, splat_influences, 
         warm_up(WU[1])
         nc.vector.tensor_copy(out=bias[:], in_=bp[:])
         regroup_w(0, 1)
-        flow_copy(0)
         regroup_w(1, 1)
+        flow_copy(0)
         quant_w(0, 1)
         quant_w(1, 1)
         transposes(2, [0, 1, 2, 3])
         transposes(3, [0, 1, 2, 3])
         add_bias(0, 0)
         add_bias(1, 0)
+        flow_copy(1)
         exit_x(2)
         exit_x(3)
-        for i in range(1, EF):
+        for i in range(2, EF):
             flow_copy(i)
         mx(0, 1)
         mx(1, 1)
@@ -319,22 +327,33 @@ def tile_splatinformationflow_pb_kernel(tc, token_embeddings, splat_influences, 
             if 0 <= sg < NT - 1:
                 sigmoid(sg, 0, D)
             if t == NT - 1:
+                fc = fcp.tile([P, H], F32, name="fc", tag="fc")
+                nc.scalar.copy(out=fc[:, 0:D - 768], in_=state[("f", t, 1)][:, 768 - H:H])
                 sigmoid(t, 0, H)
                 sigmoid(t, H, D)
             for i in fs[1:]:
                 flow_copy(i)
             if has_m:
                 mult_v(u, 0)
-                if u >= NT - TAIL:
-                    store(u, 0, H)
-                if u > NT - TAIL:
+                if u == NT - 2:
                     store(u - 1, H, D)
+                    store(u - 1, 0, H)
+                    store(u, 0, H)
+                if u == NT - 1:
+                    store(u - 1, H, D)
+                    store(u, 0, H)
                 if on_g:
                     mult_g(u)
+                elif u == NT - 1:
+                    z = state[("z", u)]
+                    o = state[("o", u)]
+                    nc.gpsimd.tensor_tensor(out=o[:, 768:D], in0=z[:, 768:D], in1=fc[:, 0:D - 768], op=ALU.mult)
+                    nc.vector.tensor_tensor(out=o[:, H:768], in0=state[("f", u, 1)][:, 0:768 - H], in1=z[:, H:768], op=ALU.mult)
                 else:
                     mult_v(u, 1)
                 if u == NT - 1:
-                    store(u, H, D)
+                    store(u, 768, D)
+                    store(u, H, 768)
                 elif u < NT - TAIL:
                     store(u, 0, D)
             if t % 4 == 0:
@@ -343,5 +362,5 @@ def tile_splatinformationflow_pb_kernel(tc, token_embeddings, splat_influences, 
                     load_x(4 * m, 4)
                     if m % 2 == 0:
                         load_small(m // 2)
-            if t % J == 2 and t // J + 1 < NB:
+            if t % J == 4 and t // J + 1 < NB:
                 infl_T(t // J + 1, True)

@@ -26,7 +26,7 @@ LF = 2
 AF = 2
 AS = 1
 TAIL = 3
-WU = (10, 3)
+WU = (8, 3)
 EF = 3
 PRE = 4
 NOG = (7, 15, 23, NT - 1)
@@ -224,9 +224,9 @@ def tile_splatinformationflow_pb_kernel(tc, token_embeddings, splat_influences, 
         masks.make_identity(nc, idb[:])
         load_w(0, 0)
         load_w(1, 0)
+        load_x(0, 1)
         load_w(2, 0)
         load_w(3, 0)
-        load_x(0, 1)
         load_x(1, 1)
         load_small(0)
         load_w(0, 1)
@@ -247,18 +247,18 @@ def tile_splatinformationflow_pb_kernel(tc, token_embeddings, splat_influences, 
 
         regroup_w(0, 0)
         quant_w(0, 0)
-        regroup_w(1, 0)
-        quant_w(1, 0)
         warm_up(WU[0])
         transposes(0, [0, 1, 2, 3])
-        warm_up(1)
+        exit_x(0)
+        regroup_w(1, 0)
+        quant_x(0, 1)
+        quant_w(1, 0)
+        warm_up(2)
         transposes(1, [0, 1, 2, 3])
         bp = ps_v.tile([P, D], BF16, name="bp", tag="b")
         for h in range(2):
             nc.tensor.matmul(out=bp[:, h * H:(h + 1) * H], lhsT=ones[:], rhs=brow[:, h * H:(h + 1) * H], start=True, stop=True)
-        exit_x(0)
         exit_x(1)
-        quant_x(0, 1)
         quant_x(1, 1)
         infl_T(0, False)
         mx(0, 0)
@@ -317,9 +317,6 @@ def tile_splatinformationflow_pb_kernel(tc, token_embeddings, splat_influences, 
             if 2 <= t < NT:
                 add_bias(t, 0)
                 add_bias(t, 1)
-            for i in range(PRE, NT, 2):
-                if t_period(i) + 2 == t:
-                    quant_x(i, 2)
             for i in es:
                 exit_x(i)
             if fs:
@@ -364,3 +361,5 @@ def tile_splatinformationflow_pb_kernel(tc, token_embeddings, splat_influences, 
                         load_small(m // 2)
             if t % J == 4 and t // J + 1 < NB:
                 infl_T(t // J + 1, True)
+            if es:
+                quant_x(es[0], 2)

@@ -22,11 +22,11 @@ FLOPS = 2 * 4096 * 1024 * 1024 + 2 * 4096 * 128 * 1024
 
 MANUAL = True
 LT = 4
-LF = 2
+LF = 1
 AF = 2
 AS = 1
 TAIL = 3
-WU = (8, 3)
+WU = (6, 3)
 EF = 3
 PRE = 4
 NOG = (7, 15, 23, NT - 1)
@@ -100,7 +100,8 @@ def tile_splatinformationflow_pb_kernel(tc, token_embeddings, splat_influences, 
 
         def regroup_w(g, h):
             base = (2 * h + g) * 2048
-            for lo, hi, eng in ((0, VSPLIT, "v"), (VSPLIT, H, "s")):
+            vs = 416 if (g, h) == (1, 0) else VSPLIT
+            for lo, hi, eng in ((0, vs, "v"), (vs, H, "s")):
                 dst = wgrp[:, base + 4 * lo:base + 4 * hi].rearrange("p (c i t) -> p c t i", i=4, t=4)
                 src = wraw[h][:, 4 * g:4 * g + 4, lo:hi].rearrange("p t (c i) -> p c t i", i=4)
                 if eng == "v":
@@ -324,8 +325,6 @@ def tile_splatinformationflow_pb_kernel(tc, token_embeddings, splat_influences, 
             if 0 <= sg < NT - 1:
                 sigmoid(sg, 0, D)
             if t == NT - 1:
-                fc = fcp.tile([P, H], F32, name="fc", tag="fc")
-                nc.scalar.copy(out=fc[:, 0:D - 768], in_=state[("f", t, 1)][:, 768 - H:H])
                 sigmoid(t, 0, H)
                 sigmoid(t, H, D)
             for i in fs[1:]:
@@ -341,16 +340,10 @@ def tile_splatinformationflow_pb_kernel(tc, token_embeddings, splat_influences, 
                     store(u, 0, H)
                 if on_g:
                     mult_g(u)
-                elif u == NT - 1:
-                    z = state[("z", u)]
-                    o = state[("o", u)]
-                    nc.gpsimd.tensor_tensor(out=o[:, 768:D], in0=z[:, 768:D], in1=fc[:, 0:D - 768], op=ALU.mult)
-                    nc.vector.tensor_tensor(out=o[:, H:768], in0=state[("f", u, 1)][:, 0:768 - H], in1=z[:, H:768], op=ALU.mult)
                 else:
                     mult_v(u, 1)
                 if u == NT - 1:
-                    store(u, 768, D)
-                    store(u, H, 768)
+                    store(u, H, D)
                 elif u < NT - TAIL:
                     store(u, 0, D)
             if t % 4 == 0:

from contextlib import ExitStack

import concourse.masks as masks
import concourse.mybir as mybir

F32 = mybir.dt.float32
BF16 = mybir.dt.bfloat16
U32 = mybir.dt.uint32
U8 = mybir.dt.uint8
I32 = mybir.dt.int32
FP8X4 = mybir.dt.float8_e4m3fn_x4
ALU = mybir.AluOpType
ACT = mybir.ActivationFunctionType

P = 128
NB = 4
J = 8
NT = NB * J
D = 1024
H = 512
FLOPS = 2 * 4096 * 1024 * 1024 + 2 * 4096 * 128 * 1024

MANUAL = True
LT = 4
LF = 1
AF = 2
AS = 1
TAIL = 3
WU = (6, 3)
EF = 3
PRE = 4
NOG = (7, 15, 23, NT - 1)
VTP = (NT - 2,)
VSPLIT = 336


def e_period(i):
    return max(i - LT, (i - PRE) // 2) + 1


def t_period(i):
    return e_period(i - i % 2) - 1


def f_period(i):
    return max(i - LF, i // 2)


def tile_splatinformationflow_pb_kernel(tc, token_embeddings, splat_influences, decoded, gate_W, gate_b, out):
    nc = tc.nc
    x_dram = token_embeddings.rearrange("b (p j) k -> b p (j k)", j=J)
    i_dram = splat_influences.rearrange("b (p j) s -> b p (j s)", j=J)
    o_dram = out.rearrange("b (p j) f -> b p (j f)", j=J)
    w_dram = gate_W.rearrange("(c p e) n -> c p e n", c=4, e=2)
    b_dram = gate_b.rearrange("(o n) -> o n", o=1)

    with ExitStack() as ctx:
        keep = ctx.enter_context(tc.tile_pool(name="keep", bufs=1))
        xgp = ctx.enter_context(tc.tile_pool(name="xgp", bufs=3))
        zp = ctx.enter_context(tc.tile_pool(name="zp", bufs=5))
        fcp = ctx.enter_context(tc.tile_pool(name="fcp", bufs=6))
        op = ctx.enter_context(tc.tile_pool(name="op", bufs=6))
        ps = ctx.enter_context(tc.psum_pool(name="ps", bufs=8))
        ps_tp = ps
        ps_v = ps
        ps_f = ps
        ps_g = ps
        if MANUAL:
            ctx.enter_context(tc.manual_schedule())

        x_sb = [keep.tile([P, J * D], BF16, name="x%d" % b) for b in range(NB)]
        i_sb = [keep.tile([P, J * P], BF16, name="i%d" % b) for b in range(NB)]
        iT_sb = [keep.tile([P, J * P], BF16, name="iT%d" % b) for b in range(NB)]
        d_sb = [keep.tile([P, D], BF16, name="d%d" % b) for b in range(NB)]
        wraw = [keep.tile([P, 8, H], BF16, name="wraw%d" % h) for h in range(2)]
        wgrp = keep.tile([P, 8 * D], BF16, name="wgrp", align_bytes=64)
        wc = keep.tile([P, 2 * D], U32, name="wc", align_bytes=64)
        ws = keep.tile([P, 2 * D], U8, name="ws", align_bytes=64)
        brow = keep.tile([P, D], BF16, name="brow")
        ones = keep.tile([P, P], BF16, name="ones")
        bias = keep.tile([P, D], BF16, name="bias")
        idf = keep.tile([P, P], F32, name="idf")
        idb = keep.tile([P, P], BF16, name="idb")
        warm = keep.tile([P, H], BF16, name="warm")
        dm = keep.tile([P, 8], F32, name="dm")
        dm2 = keep.tile([P, 8], F32, name="dm2")

        state = {}

        def load_w(c, h):
            nc.sync.dma_start(out=wraw[h][:, 2 * c:2 * c + 2, :], in_=w_dram[c, :, :, h * H:(h + 1) * H])

        def load_x(i0, n):
            b, j = divmod(i0, J)
            nc.sync.dma_start(out=x_sb[b][:, j * D:(j + n) * D], in_=x_dram[b, :, j * D:(j + n) * D])

        def load_small(b):
            nc.sync.dma_start(out=i_sb[b][:], in_=i_dram[b])
            nc.sync.dma_start(out=d_sb[b][:], in_=decoded[b])

        def regroup_w(g, h):
            base = (2 * h + g) * 2048
            vs = 416 if (g, h) == (1, 0) else VSPLIT
            for lo, hi, eng in ((0, vs, "v"), (vs, H, "s")):
                dst = wgrp[:, base + 4 * lo:base + 4 * hi].rearrange("p (c i t) -> p c t i", i=4, t=4)
                src = wraw[h][:, 4 * g:4 * g + 4, lo:hi].rearrange("p t (c i) -> p c t i", i=4)
                if eng == "v":
                    nc.vector.tensor_copy(out=dst, in_=src)
                else:
                    nc.scalar.copy(out=dst, in_=src)

        def quant_w(g, h):
            r = h * D + g * H
            nc.vector.quantize_mx(
                out=wc[:, r:r + H].bitcast(FP8X4),
                scales=ws[:, r:r + H],
                in_=wgrp[:, 4 * r:4 * (r + H)],
            )

        def transposes(i, cs):
            b, j = divmod(i, J)
            if 0 in cs:
                xt = ps_tp.tile([P, 4, P], F32, name="xt", tag="b")
                state[("xt", i)] = xt
            xt = state[("xt", i)]
            xw = x_sb[b][:].bitcast(F32)
            for c in cs:
                nc.tensor.transpose(xt[:, c, :], xw[:, j * H + c * P:j * H + (c + 1) * P], idf[:])

        def exit_x(i):
            m, r = divmod(i, 2)
            if r == 0:
                xg = xgp.tile([P, 2 * D], BF16, name="xg", tag="xg", align_bytes=64)
                xc = xgp.tile([P, 512], U32, name="xc", tag="xc", align_bytes=64)
                xs = xgp.tile([P, 512], U8, name="xs", tag="xs", align_bytes=64)
                state[("xq", m)] = (xg, xc, xs)
            xg = state[("xq", m)][0]
            nc.scalar.copy(
                out=xg[:, r * D:(r + 1) * D].bitcast(F32).rearrange("p (g r u) -> p g r u", g=2, u=2),
                in_=state[("xt", i)][:].rearrange("p (g u) r -> p g r u", u=2),
            )

        def quant_x(i, n):
            m, r = divmod(i, 2)
            xg, xc, xs = state[("xq", m)]
            nc.vector.quantize_mx(
                out=xc[:, r * 256:(r + n) * 256].bitcast(FP8X4),
                scales=xs[:, r * 256:(r + n) * 256],
                in_=xg[:, r * D:(r + n) * D],
            )

        def infl_T(b, on_vector):
            it = ps_tp.tile([P, J * P], BF16, name="it", tag="b")
            for j in range(J):
                nc.tensor.transpose(it[:, j * P:(j + 1) * P], i_sb[b][:, j * P:(j + 1) * P], idb[:])
            if on_vector:
                nc.vector.tensor_copy(out=iT_sb[b][:], in_=it[:])
            else:
                nc.scalar.copy(out=iT_sb[b][:], in_=it[:])

        def mx(i, h):
            xc, xs = state[("xq", i // 2)][1:]
            x0 = (i % 2) * 256
            if i in VTP:
                v = ps_tp.tile([P, H], F32, name="vt", tag="b")
            else:
                v = ps_v.tile([P, H], F32, name="v", tag="b")
            state[("v", i, h)] = v
            for g in range(2):
                r = h * D + g * H
                nc.tensor.matmul_mx(
                    out=v[:],
                    lhsT=xc[:, x0 + g * P:x0 + (g + 1) * P].bitcast(FP8X4),
                    lhsT_scale=xs[:, x0 + g * P:x0 + (g + 1) * P],
                    rhs=wc[:, r:r + H].bitcast(FP8X4),
                    rhs_scale=ws[:, r:r + H],
                    start=(g == 0),
                    stop=(g == 1),
                )

        def add_bias(i, h):
            if h == 0:
                z = zp.tile([P, D], F32, name="z", tag="z")
                state[("z", i)] = z
            z = state[("z", i)]
            nc.vector.tensor_tensor(out=z[:, h * H:(h + 1) * H], in0=state[("v", i, h)][:], in1=bias[:, h * H:(h + 1) * H], op=ALU.add)

        def sigmoid(i, lo, hi):
            z = state[("z", i)]
            nc.scalar.activation(out=z[:, lo:hi], in_=z[:, lo:hi], func=ACT.Sigmoid)

        def flow(i, h, pool, tag):
            b, j = divmod(i, J)
            f = pool.tile([P, H], F32, name=tag, tag="b")
            state[("f", i, h)] = f
            nc.tensor.matmul(out=f[:], lhsT=iT_sb[b][:, j * P:(j + 1) * P], rhs=d_sb[b][:, h * H:(h + 1) * H], start=True, stop=True)

        def flow_copy(i):
            fc = fcp.tile([P, H], F32, name="fc", tag="fc")
            state[("fc", i)] = fc
            nc.scalar.copy(out=fc[:], in_=state[("f", i, 1)][:])

        def mult_v(i, h):
            if h == 0:
                o = op.tile([P, D], F32, name="o", tag="o")
                state[("o", i)] = o
            o = state[("o", i)]
            nc.vector.tensor_tensor(out=o[:, h * H:(h + 1) * H], in0=state[("f", i, h)][:], in1=state[("z", i)][:, h * H:(h + 1) * H], op=ALU.mult)

        def mult_g(i):
            o = state[("o", i)]
            nc.gpsimd.tensor_tensor(out=o[:, H:D], in0=state[("z", i)][:, H:D], in1=state[("fc", i)][:], op=ALU.mult)

        def store(i, lo, hi):
            b, j = divmod(i, J)
            nc.sync.dma_start(out=o_dram[b, :, j * D + lo:j * D + hi], in_=state[("o", i)][:, lo:hi])

        nc.vector.memset(brow[:].bitcast(I32), 0)
        nc.vector.memset(ones[:], 1.0)
        nc.vector.memset(warm[:], 0.0)
        nc.vector.memset(dm[:], 0.0)
        nc.scalar.dma_start(out=brow[0:1, :], in_=b_dram)
        nc.scalar.activation(out=dm2[:], in_=dm[:], func=ACT.Sigmoid)
        masks.make_identity(nc, idf[:])
        masks.make_identity(nc, idb[:])
        load_w(0, 0)
        load_w(1, 0)
        load_x(0, 1)
        load_w(2, 0)
        load_w(3, 0)
        load_x(1, 1)
        load_small(0)
        load_w(0, 1)
        load_w(1, 1)
        load_w(2, 1)
        load_w(3, 1)
        load_x(2, 1)
        load_x(3, 1)
        load_x(4, 2)
        load_x(6, 2)
        load_x(8, 4)
        load_small(1)

        def warm_up(n):
            wu = ps.tile([P, H], F32, name="wu", tag="b")
            for q in range(n):
                nc.tensor.matmul(out=wu[:], lhsT=ones[:], rhs=warm[:], start=True, stop=True)

        regroup_w(0, 0)
        quant_w(0, 0)
        warm_up(WU[0])
        transposes(0, [0, 1, 2, 3])
        exit_x(0)
        regroup_w(1, 0)
        quant_x(0, 1)
        quant_w(1, 0)
        warm_up(2)
        transposes(1, [0, 1, 2, 3])
        bp = ps_v.tile([P, D], BF16, name="bp", tag="b")
        for h in range(2):
            nc.tensor.matmul(out=bp[:, h * H:(h + 1) * H], lhsT=ones[:], rhs=brow[:, h * H:(h + 1) * H], start=True, stop=True)
        exit_x(1)
        quant_x(1, 1)
        infl_T(0, False)
        mx(0, 0)
        mx(1, 0)
        for i in range(EF):
            flow(i, 1, ps_f, "f")
        warm_up(WU[1])
        nc.vector.tensor_copy(out=bias[:], in_=bp[:])
        regroup_w(0, 1)
        regroup_w(1, 1)
        flow_copy(0)
        quant_w(0, 1)
        quant_w(1, 1)
        transposes(2, [0, 1, 2, 3])
        transposes(3, [0, 1, 2, 3])
        add_bias(0, 0)
        add_bias(1, 0)
        flow_copy(1)
        exit_x(2)
        exit_x(3)
        for i in range(2, EF):
            flow_copy(i)
        mx(0, 1)
        mx(1, 1)
        quant_x(2, 2)
        add_bias(0, 1)
        add_bias(1, 1)

        for t in range(NT + AF):
            u = t - AF
            has_m = 0 <= u < NT
            on_g = has_m and u not in NOG
            sg = t - AS
            ts = [i for i in range(PRE, NT) if t_period(i) == t]
            es = [i for i in range(PRE, NT) if t_period(i) + 1 == t]
            fs = [i for i in range(EF, NT) if f_period(i) == t and i not in NOG]
            if fs:
                flow(fs[0], 1, ps_g, "fg")
            for i in fs[1:]:
                flow(i, 1, ps_f, "f")
            if 2 <= t < NT:
                mx(t, 0)
                mx(t, 1)
            if has_m and u < NT - 2:
                flow(u, 0, ps_f, "f")
                if not on_g:
                    flow(u, 1, ps_f, "f")
            if t == NT - 1:
                flow(NT - 2, 0, ps_f, "f")
                flow(NT - 1, 0, ps_tp, "tp")
                flow(NT - 1, 1, ps_g, "fg")
            if ts:
                transposes(ts[0], [0, 1, 2, 3])
            for i in ts[1:]:
                transposes(i, [0, 1, 2, 3])
            if 2 <= t < NT:
                add_bias(t, 0)
                add_bias(t, 1)
            for i in es:
                exit_x(i)
            if fs:
                flow_copy(fs[0])
            if 0 <= sg < NT - 1:
                sigmoid(sg, 0, D)
            if t == NT - 1:
                sigmoid(t, 0, H)
                sigmoid(t, H, D)
            for i in fs[1:]:
                flow_copy(i)
            if has_m:
                mult_v(u, 0)
                if u == NT - 2:
                    store(u - 1, H, D)
                    store(u - 1, 0, H)
                    store(u, 0, H)
                if u == NT - 1:
                    store(u - 1, H, D)
                    store(u, 0, H)
                if on_g:
                    mult_g(u)
                else:
                    mult_v(u, 1)
                if u == NT - 1:
                    store(u, H, D)
                elif u < NT - TAIL:
                    store(u, 0, D)
            if t % 4 == 0:
                m = (t + 12) // 4
                if m < NT // 4:
                    load_x(4 * m, 4)
                    if m % 2 == 0:
                        load_small(m // 2)
            if t % J == 4 and t // J + 1 < NB:
                infl_T(t // J + 1, True)
            if es:
                quant_x(es[0], 2)
